import numpy as np
import ml_dtypes


def mxq(x, axis, fmt="e4m3"):
    dtype, down = {"e4m3": (ml_dtypes.float8_e4m3fn, 7), "e5m2": (ml_dtypes.float8_e5m2, 14)}[fmt]
    v = np.moveaxis(np.asarray(x, np.float32).astype(ml_dtypes.bfloat16).astype(np.float64), axis, -1)
    blocks = v.reshape(v.shape[:-1] + (-1, 32))
    amax = np.abs(blocks).max(-1, keepdims=True)
    byte = np.maximum(np.where(amax > 0, np.frexp(amax)[1] - 1 + 127, 0) - down, 1)
    scale = np.exp2(byte - 127.0)
    codes = (blocks / scale).astype(np.float32).astype(dtype).astype(np.float64)
    return np.moveaxis((codes * scale).reshape(v.shape), -1, axis)


WIDE = False


def mx_kscale(k):
    if not WIDE:
        return np.ones(k)
    levels = np.array([10, -10, 5, -5, 0])
    if k % 512:
        return np.exp2(np.random.permutation(np.resize(levels, k // 32))).repeat(32)
    a = np.empty((k // 512, 16))
    for p in range(k // 512):
        a[p, :8] = np.random.permutation(np.resize(levels, 8))
        for g in range(8):
            far = levels[np.abs(levels - a[p, g]) >= 10]
            a[p, g + 8] = far[np.random.randint(len(far))]
    return np.exp2(a.ravel()).repeat(32)


BF16 = ml_dtypes.bfloat16


def bf(x):
    return np.asarray(x, np.float32).astype(BF16)


def f64(x):
    return np.asarray(x).astype(np.float64)


B, S, D, NH = 2, 64, 1024, 8
SCALE = np.sqrt(D // NH)


def setup_inputs():
    s, t = mx_kscale(D), mx_kscale(D)
    return {"x": bf(np.random.standard_normal((B, S, D)) * s),
            "wq": bf(np.random.standard_normal((D, D)) * 0.84 / np.sqrt(D) / s[None, :] * t[:, None]),
            "wk": bf(np.random.standard_normal((D, D)) * 0.84 / np.sqrt(D) / s[None, :] / t[:, None])}


def reference(x, wq, wk):
    xq = mxq(f64(x), 2, "e4m3")
    q = xq @ mxq(f64(wq), 1, "e4m3").T
    k = xq @ mxq(f64(wk), 1, "e4m3").T
    sc = (mxq(q, 2, "e4m3") @ mxq(k, 2, "e4m3").transpose(0, 2, 1)) / SCALE
    e = np.exp(sc - sc.max(-1, keepdims=True))
    return e / e.sum(-1, keepdims=True)

@@ -1,0 +1,164 @@
+from contextlib import ExitStack
+import math
+
+import concourse.masks as masks
+import concourse.mybir as mybir
+
+F32 = mybir.dt.float32
+BF16 = mybir.dt.bfloat16
+U32 = mybir.dt.uint32
+U8 = mybir.dt.uint8
+FP8X4 = mybir.dt.float8_e4m3fn_x4
+
+P = 128
+PACK = 4
+K_PASS = P * PACK
+BATCH, SEQ, D = 2, 64, 1024
+TOKENS = BATCH * SEQ
+PASSES = D // K_PASS
+WORDS = D // 2
+BLOCKS = WORDS // P
+INV_SQRT = 1.0 / math.sqrt(D // 8)
+
+FLOPS = 2 * 2 * TOKENS * D * D + 2 * BATCH * SEQ * SEQ * D
+
+
+def tile_attentionnet_pa_s_kernel(tc, x, wq, wk, out):
+    nc = tc.nc
+    weights = {"q": wq, "k": wk}
+    with ExitStack() as ctx:
+        keep = ctx.enter_context(tc.tile_pool(name="keep", bufs=1))
+        turned_pool = ctx.enter_context(tc.psum_pool(name="turned", bufs=5))
+        proj_pool = ctx.enter_context(tc.psum_pool(name="proj", bufs=2))
+        score_pool = ctx.enter_context(tc.psum_pool(name="score", bufs=1))
+        ctx.enter_context(tc.manual_schedule())
+
+        x_rows = keep.tile([P, D], BF16, name="x_rows")
+        x_grouped = keep.tile([P, D], BF16, name="x_grouped", align_bytes=64)
+        x_codes = keep.tile([P, PASSES, TOKENS], U32, name="x_codes", align_bytes=64)
+        x_scales = keep.tile([P, PASSES, TOKENS], U8, name="x_scales", align_bytes=64)
+        w_rows, w_grouped, w_codes, w_scales = {}, {}, {}, {}
+        f_grouped, f_codes, f_scales = {}, {}, {}
+        for n in weights:
+            w_rows[n] = keep.tile([P, PASSES, PACK, D], BF16, name="rows_" + n)
+            w_grouped[n] = keep.tile([P, PASSES, PACK, D], BF16, name="grouped_" + n, align_bytes=64)
+            w_codes[n] = keep.tile([P, PASSES, PACK, PASSES, P], U32, name="codes_" + n, align_bytes=64)
+            w_scales[n] = keep.tile([P, PASSES, PACK, PASSES, P], U8, name="scales_" + n, align_bytes=64)
+            f_grouped[n] = keep.tile([P, PASSES, TOKENS, PACK], BF16, name="fgrouped_" + n, align_bytes=64)
+            f_codes[n] = keep.tile([P, PASSES, TOKENS], U32, name="fcodes_" + n, align_bytes=64)
+            f_scales[n] = keep.tile([P, PASSES, TOKENS], U8, name="fscales_" + n, align_bytes=64)
+
+        nc.sync.dma_start(out=x_rows[:], in_=x.rearrange("b s d -> (b s) d"))
+        chunks = [(n, g) for g in range(PASSES) for n in ("q", "k")]
+        for i, (n, g) in enumerate(chunks):
+            view = weights[n].rearrange("(g p t) d -> p g t d", g=PASSES, p=P, t=PACK)
+            for t0 in range(0, PACK, 2):
+                at_an_end = (i == 0 and t0 == 0) or (i == len(chunks) - 1 and t0 == PACK - 2)
+                step = 1 if at_an_end else 2
+                for t in range(t0, t0 + 2, step):
+                    nc.sync.dma_start(out=w_rows[n][:, g, t : t + step, :], in_=view[:, g, t : t + step, :])
+
+        ident = keep.tile([P, P], F32, name="ident")
+        masks.make_identity(nc, ident[:])
+
+        zero = keep.tile([P, 1], F32, name="zero")
+        one = keep.tile([P, 1], F32, name="one")
+        nc.vector.memset(zero[:], 0.0)
+        nc.scalar.activation(out=one[:], in_=zero[:], func=mybir.ActivationFunctionType.Exp)
+
+        def turn(rows, grouped, copy):
+            turned = turned_pool.tile([P, BLOCKS, P], F32, name="turned")
+            words = rows.bitcast(F32)
+            for c in range(PASSES):
+                for u in range(2):
+                    picked = words[:, c * 2 * P + u : (c + 1) * 2 * P : 2]
+                    nc.tensor.transpose(turned[:, 2 * c + u, :], picked, ident[:])
+            copy(
+                out=grouped.bitcast(F32).rearrange("p (c m u) -> p c m u", c=PASSES, u=2),
+                in_=turned[:].rearrange("p (c u) m -> p c m u", u=2),
+            )
+
+        def quantise(grouped, codes, scales):
+            nc.vector.quantize_mx(out=codes.bitcast(FP8X4), scales=scales, in_=grouped)
+
+        def front(n, g):
+            for t in range(PACK):
+                copy = nc.vector.tensor_copy if t == 1 else nc.scalar.copy
+                turn(w_rows[n][:, g, t, :], w_grouped[n][:, g, t, :], copy)
+                if t > 0:
+                    quantise_rows(n, g, t - 1)
+            quantise_rows(n, g, PACK - 1)
+
+        def quantise_rows(n, g, t):
+            quantise(
+                w_grouped[n][:, g, t, :],
+                w_codes[n][:, g, t, :, :].rearrange("p c m -> p (c m)"),
+                w_scales[n][:, g, t, :, :].rearrange("p c m -> p (c m)"),
+            )
+
+        def back(n, g):
+            proj = proj_pool.tile([P, PACK, TOKENS], F32, name="proj")
+            for t in range(PACK):
+                for c in range(PASSES):
+                    nc.tensor.matmul_mx(
+                        out=proj[:, t, :],
+                        lhsT=w_codes[n][:, g, t, c, :].bitcast(FP8X4),
+                        lhsT_scale=w_scales[n][:, g, t, c, :],
+                        rhs=x_codes[:, c, :].bitcast(FP8X4),
+                        rhs_scale=x_scales[:, c, :],
+                        start=(c == 0),
+                        stop=(c == PASSES - 1),
+                    )
+            nc.scalar.copy(out=f_grouped[n][:, g, :, :], in_=proj[:].rearrange("p t n -> p n t"))
+            quantise(
+                f_grouped[n][:, g, :, :].rearrange("p n t -> p (n t)"),
+                f_codes[n][:, g, :],
+                f_scales[n][:, g, :],
+            )
+
+        turn(x_rows[:], x_grouped[:], nc.vector.tensor_copy)
+        quantise(
+            x_grouped[:],
+            x_codes[:].rearrange("p c m -> p (c m)"),
+            x_scales[:].rearrange("p c m -> p (c m)"),
+        )
+        front(*chunks[0])
+        for i in range(1, len(chunks)):
+            front(*chunks[i])
+            back(*chunks[i - 1])
+        back(*chunks[-1])
+
+        scores = score_pool.tile([P, TOKENS], F32, name="scores")
+        for g in range(PASSES):
+            nc.tensor.matmul_mx(
+                out=scores[:],
+                lhsT=f_codes["q"][:, g, :].bitcast(FP8X4),
+                lhsT_scale=f_scales["q"][:, g, :],
+                rhs=f_codes["k"][:, g, :].bitcast(FP8X4),
+                rhs_scale=f_scales["k"][:, g, :],
+                start=(g == 0),
+                stop=(g == PASSES - 1),
+            )
+
+        scaled = keep.tile([P, SEQ], F32, name="scaled")
+        nc.vector.tensor_scalar_mul(out=scaled[0:SEQ, :], in0=scores[0:SEQ, 0:SEQ], scalar1=INV_SQRT)
+        nc.vector.tensor_scalar_mul(out=scaled[SEQ:P, :], in0=scores[SEQ:P, SEQ:P], scalar1=INV_SQRT)
+        neg_max = keep.tile([P, 1], F32, name="neg_max")
+        nc.vector.tensor_reduce(
+            out=neg_max[:], in_=scaled[:], axis=mybir.AxisListType.X, op=mybir.AluOpType.max, negate=True
+        )
+        expd = keep.tile([P, SEQ], F32, name="expd")
+        row_sum = keep.tile([P, 1], F32, name="row_sum")
+        nc.scalar.activation(
+            out=expd[:],
+            in_=scaled[:],
+            func=mybir.ActivationFunctionType.Exp,
+            bias=neg_max[:, 0:1],
+            scale=1.0,
+            accum_out=row_sum[:],
+        )
+        inv_sum = keep.tile([P, 1], F32, name="inv_sum")
+        nc.vector.reciprocal(out=inv_sum[:], in_=row_sum[:])
+        prob = keep.tile([P, SEQ], F32, name="prob")
+        nc.vector.tensor_scalar_mul(out=prob[:], in0=expd[:], scalar1=inv_sum[:, 0:1])
+        nc.sync.dma_start(out=out.rearrange("b s k -> (b s) k"), in_=prob[:])

@@ -48,15 +48,15 @@ def tile_attentionnet_pa_s_kernel(tc, x, wq, wk, out):
             f_codes[n] = keep.tile([P, PASSES, TOKENS], U32, name="fcodes_" + n, align_bytes=64)
             f_scales[n] = keep.tile([P, PASSES, TOKENS], U8, name="fscales_" + n, align_bytes=64)
 
-        nc.sync.dma_start(out=x_rows[:], in_=x.rearrange("b s d -> (b s) d"))
+        x_view = x.rearrange("b s d -> (b s) d")
+        for c in range(PASSES):
+            half = slice(c * K_PASS, (c + 1) * K_PASS)
+            nc.sync.dma_start(out=x_rows[:, half], in_=x_view[:, half])
         chunks = [(n, g) for g in range(PASSES) for n in ("q", "k")]
-        for i, (n, g) in enumerate(chunks):
+        for n, g in chunks:
             view = weights[n].rearrange("(g p t) d -> p g t d", g=PASSES, p=P, t=PACK)
-            for t0 in range(0, PACK, 2):
-                at_an_end = (i == 0 and t0 == 0) or (i == len(chunks) - 1 and t0 == PACK - 2)
-                step = 1 if at_an_end else 2
-                for t in range(t0, t0 + 2, step):
-                    nc.sync.dma_start(out=w_rows[n][:, g, t : t + step, :], in_=view[:, g, t : t + step, :])
+            for t in range(PACK):
+                nc.sync.dma_start(out=w_rows[n][:, g, t, :], in_=view[:, g, t, :])
 
         ident = keep.tile([P, P], F32, name="ident")
         masks.make_identity(nc, ident[:])
@@ -96,25 +96,75 @@ def tile_attentionnet_pa_s_kernel(tc, x, wq, wk, out):
                 w_scales[n][:, g, t, :, :].rearrange("p c m -> p (c m)"),
             )
 
-        def back(n, g):
-            proj = proj_pool.tile([P, PACK, TOKENS], F32, name="proj")
-            for t in range(PACK):
-                for c in range(PASSES):
-                    nc.tensor.matmul_mx(
-                        out=proj[:, t, :],
-                        lhsT=w_codes[n][:, g, t, c, :].bitcast(FP8X4),
-                        lhsT_scale=w_scales[n][:, g, t, c, :],
-                        rhs=x_codes[:, c, :].bitcast(FP8X4),
-                        rhs_scale=x_scales[:, c, :],
-                        start=(c == 0),
-                        stop=(c == PASSES - 1),
-                    )
-            nc.scalar.copy(out=f_grouped[n][:, g, :, :], in_=proj[:].rearrange("p t n -> p n t"))
+        def last_front(n, g):
+            for t in range(PACK - 1):
+                copy = nc.vector.tensor_copy if t == 1 else nc.scalar.copy
+                turn(w_rows[n][:, g, t, :], w_grouped[n][:, g, t, :], copy)
+                if t > 0:
+                    quantise_rows(n, g, t - 1)
+            t = PACK - 1
+            words = w_rows[n][:, g, t, :].bitcast(F32)
+            grouped = w_grouped[n][:, g, t, :].rearrange("p (c k) -> p c k", c=PASSES)
+            halves = []
+            for c in range(PASSES):
+                turned = turned_pool.tile([P, BLOCKS, P], F32, name="turned")
+                for u in range(2):
+                    picked = words[:, c * 2 * P + u : (c + 1) * 2 * P : 2]
+                    nc.tensor.transpose(turned[:, u, :], picked, ident[:])
+                halves.append(turned)
+            for c, copy in enumerate((nc.vector.tensor_copy, nc.scalar.copy)):
+                copy(
+                    out=grouped[:, c, :].bitcast(F32).rearrange("p (m u) -> p m u", u=2),
+                    in_=halves[c][:, 0:2, :].rearrange("p u m -> p m u"),
+                )
+            quantise_rows(n, g, t - 1)
+            for c in range(PASSES):
+                quantise(grouped[:, c, :], w_codes[n][:, g, t, c, :], w_scales[n][:, g, t, c, :])
+
+        def quantise_features(n, g):
             quantise(
                 f_grouped[n][:, g, :, :].rearrange("p n t -> p (n t)"),
                 f_codes[n][:, g, :],
                 f_scales[n][:, g, :],
             )
+
+        def project(n, g, t, out):
+            for c in range(PASSES):
+                nc.tensor.matmul_mx(
+                    out=out,
+                    lhsT=w_codes[n][:, g, t, c, :].bitcast(FP8X4),
+                    lhsT_scale=w_scales[n][:, g, t, c, :],
+                    rhs=x_codes[:, c, :].bitcast(FP8X4),
+                    rhs_scale=x_scales[:, c, :],
+                    start=(c == 0),
+                    stop=(c == PASSES - 1),
+                )
+
+        def back(n, g):
+            proj = proj_pool.tile([P, PACK, TOKENS], F32, name="proj")
+            for t in range(PACK):
+                project(n, g, t, proj[:, t, :])
+            nc.scalar.copy(out=f_grouped[n][:, g, :, :], in_=proj[:].rearrange("p t n -> p n t"))
+            quantise_features(n, g)
+
+        def last_backs(before, last):
+            n, g = before
+            proj = proj_pool.tile([P, PACK, TOKENS], F32, name="proj")
+            for t in range(PACK):
+                project(n, g, t, proj[:, t, :])
+            nc.scalar.copy(out=f_grouped[n][:, g, :, :], in_=proj[:].rearrange("p t n -> p n t"))
+            n, g = last
+            for t0, copy in ((0, nc.vector.tensor_copy), (2, nc.scalar.copy)):
+                part = turned_pool.tile([P, BLOCKS, P], F32, name="turned")
+                for t in range(t0, t0 + 2):
+                    project(n, g, t, part[:, t - t0, :])
+                copy(
+                    out=f_grouped[n][:, g, :, t0 : t0 + 2],
+                    in_=part[:, 0:2, :].rearrange("p t n -> p n t"),
+                )
+                if t0 == 0:
+                    quantise_features(*before)
+            quantise_features(*last)
 
         turn(x_rows[:], x_grouped[:], nc.vector.tensor_copy)
         quantise(
@@ -124,9 +174,10 @@ def tile_attentionnet_pa_s_kernel(tc, x, wq, wk, out):
         )
         front(*chunks[0])
         for i in range(1, len(chunks)):
-            front(*chunks[i])
-            back(*chunks[i - 1])
-        back(*chunks[-1])
+            (front if i < len(chunks) - 1 else last_front)(*chunks[i])
+            if i < len(chunks) - 1:
+                back(*chunks[i - 1])
+        last_backs(chunks[-2], chunks[-1])
 
         scores = score_pool.tile([P, TOKENS], F32, name="scores")
         for g in range(PASSES):
@@ -141,12 +192,18 @@ def tile_attentionnet_pa_s_kernel(tc, x, wq, wk, out):
             )
 
         scaled = keep.tile([P, SEQ], F32, name="scaled")
-        nc.vector.tensor_scalar_mul(out=scaled[0:SEQ, :], in0=scores[0:SEQ, 0:SEQ], scalar1=INV_SQRT)
-        nc.vector.tensor_scalar_mul(out=scaled[SEQ:P, :], in0=scores[SEQ:P, SEQ:P], scalar1=INV_SQRT)
         neg_max = keep.tile([P, 1], F32, name="neg_max")
-        nc.vector.tensor_reduce(
-            out=neg_max[:], in_=scaled[:], axis=mybir.AxisListType.X, op=mybir.AluOpType.max, negate=True
-        )
+        for b in range(BATCH):
+            rows = slice(b * SEQ, (b + 1) * SEQ)
+            nc.vector.tensor_scalar(
+                out=scaled[rows, :],
+                in0=scores[rows, rows],
+                scalar1=-INV_SQRT,
+                scalar2=None,
+                op0=mybir.AluOpType.mult,
+                op1=mybir.AluOpType.min,
+                accum_out=neg_max[rows, :],
+            )
         expd = keep.tile([P, SEQ], F32, name="expd")
         row_sum = keep.tile([P, 1], F32, name="row_sum")
         nc.scalar.activation(
@@ -154,7 +211,7 @@ def tile_attentionnet_pa_s_kernel(tc, x, wq, wk, out):
             in_=scaled[:],
             func=mybir.ActivationFunctionType.Exp,
             bias=neg_max[:, 0:1],
-            scale=1.0,
+            scale=-1.0,
             accum_out=row_sum[:],
         )
         inv_sum = keep.tile([P, 1], F32, name="inv_sum")

@@ -48,15 +48,15 @@ def tile_attentionnet_pa_s_kernel(tc, x, wq, wk, out):
             f_codes[n] = keep.tile([P, PASSES, TOKENS], U32, name="fcodes_" + n, align_bytes=64)
             f_scales[n] = keep.tile([P, PASSES, TOKENS], U8, name="fscales_" + n, align_bytes=64)
 
-        x_view = x.rearrange("b s d -> (b s) d")
-        for c in range(PASSES):
-            half = slice(c * K_PASS, (c + 1) * K_PASS)
-            nc.sync.dma_start(out=x_rows[:, half], in_=x_view[:, half])
+        nc.sync.dma_start(out=x_rows[:], in_=x.rearrange("b s d -> (b s) d"))
         chunks = [(n, g) for g in range(PASSES) for n in ("q", "k")]
-        for n, g in chunks:
+        for i, (n, g) in enumerate(chunks):
             view = weights[n].rearrange("(g p t) d -> p g t d", g=PASSES, p=P, t=PACK)
-            for t in range(PACK):
-                nc.sync.dma_start(out=w_rows[n][:, g, t, :], in_=view[:, g, t, :])
+            for t0 in range(0, PACK, 2):
+                at_an_end = (i == 0 and t0 == 0) or (i == len(chunks) - 1 and t0 == PACK - 2)
+                step = 1 if at_an_end else 2
+                for t in range(t0, t0 + 2, step):
+                    nc.sync.dma_start(out=w_rows[n][:, g, t : t + step, :], in_=view[:, g, t : t + step, :])
 
         ident = keep.tile([P, P], F32, name="ident")
         masks.make_identity(nc, ident[:])

@@ -52,11 +52,9 @@ def tile_attentionnet_pa_s_kernel(tc, x, wq, wk, out):
         chunks = [(n, g) for g in range(PASSES) for n in ("q", "k")]
         for i, (n, g) in enumerate(chunks):
             view = weights[n].rearrange("(g p t) d -> p g t d", g=PASSES, p=P, t=PACK)
-            for t0 in range(0, PACK, 2):
-                at_an_end = (i == 0 and t0 == 0) or (i == len(chunks) - 1 and t0 == PACK - 2)
-                step = 1 if at_an_end else 2
-                for t in range(t0, t0 + 2, step):
-                    nc.sync.dma_start(out=w_rows[n][:, g, t : t + step, :], in_=view[:, g, t : t + step, :])
+            step = 1 if i == 0 else 2
+            for t in range(0, PACK, step):
+                nc.sync.dma_start(out=w_rows[n][:, g, t : t + step, :], in_=view[:, g, t : t + step, :])
 
         ident = keep.tile([P, P], F32, name="ident")
         masks.make_identity(nc, ident[:])

@@ -28,8 +28,7 @@ def tile_attentionnet_pa_s_kernel(tc, x, wq, wk, out):
     weights = {"q": wq, "k": wk}
     with ExitStack() as ctx:
         keep = ctx.enter_context(tc.tile_pool(name="keep", bufs=1))
-        turned_pool = ctx.enter_context(tc.psum_pool(name="turned", bufs=5))
-        proj_pool = ctx.enter_context(tc.psum_pool(name="proj", bufs=2))
+        turned_pool = ctx.enter_context(tc.psum_pool(name="turned", bufs=7))
         score_pool = ctx.enter_context(tc.psum_pool(name="score", bufs=1))
         ctx.enter_context(tc.manual_schedule())
 
@@ -50,11 +49,10 @@ def tile_attentionnet_pa_s_kernel(tc, x, wq, wk, out):
 
         nc.sync.dma_start(out=x_rows[:], in_=x.rearrange("b s d -> (b s) d"))
         chunks = [(n, g) for g in range(PASSES) for n in ("q", "k")]
-        for i, (n, g) in enumerate(chunks):
+        for n, g in chunks:
             view = weights[n].rearrange("(g p t) d -> p g t d", g=PASSES, p=P, t=PACK)
-            step = 1 if i == 0 else 2
-            for t in range(0, PACK, step):
-                nc.sync.dma_start(out=w_rows[n][:, g, t : t + step, :], in_=view[:, g, t : t + step, :])
+            for t in range(0, PACK, 2):
+                nc.sync.dma_start(out=w_rows[n][:, g, t : t + 2, :], in_=view[:, g, t : t + 2, :])
 
         ident = keep.tile([P, P], F32, name="ident")
         masks.make_identity(nc, ident[:])
@@ -138,31 +136,14 @@ def tile_attentionnet_pa_s_kernel(tc, x, wq, wk, out):
                     stop=(c == PASSES - 1),
                 )
 
-        def back(n, g):
-            proj = proj_pool.tile([P, PACK, TOKENS], F32, name="proj")
-            for t in range(PACK):
-                project(n, g, t, proj[:, t, :])
-            nc.scalar.copy(out=f_grouped[n][:, g, :, :], in_=proj[:].rearrange("p t n -> p n t"))
-            quantise_features(n, g)
-
-        def last_backs(before, last):
-            n, g = before
-            proj = proj_pool.tile([P, PACK, TOKENS], F32, name="proj")
-            for t in range(PACK):
-                project(n, g, t, proj[:, t, :])
-            nc.scalar.copy(out=f_grouped[n][:, g, :, :], in_=proj[:].rearrange("p t n -> p n t"))
-            n, g = last
-            for t0, copy in ((0, nc.vector.tensor_copy), (2, nc.scalar.copy)):
-                part = turned_pool.tile([P, BLOCKS, P], F32, name="turned")
-                for t in range(t0, t0 + 2):
-                    project(n, g, t, part[:, t - t0, :])
-                copy(
-                    out=f_grouped[n][:, g, :, t0 : t0 + 2],
-                    in_=part[:, 0:2, :].rearrange("p t n -> p n t"),
-                )
-                if t0 == 0:
-                    quantise_features(*before)
-            quantise_features(*last)
+        def back(n, g, t0, t1, copy):
+            proj = turned_pool.tile([P, BLOCKS, P], F32, name="turned")
+            for t in range(t0, t1):
+                project(n, g, t, proj[:, t - t0, :])
+            copy(
+                out=f_grouped[n][:, g, :, t0:t1],
+                in_=proj[:, 0 : t1 - t0, :].rearrange("p t n -> p n t"),
+            )
 
         turn(x_rows[:], x_grouped[:], nc.vector.tensor_copy)
         quantise(
@@ -173,9 +154,15 @@ def tile_attentionnet_pa_s_kernel(tc, x, wq, wk, out):
         front(*chunks[0])
         for i in range(1, len(chunks)):
             (front if i < len(chunks) - 1 else last_front)(*chunks[i])
-            if i < len(chunks) - 1:
-                back(*chunks[i - 1])
-        last_backs(chunks[-2], chunks[-1])
+        back(*chunks[0], 0, PACK, nc.scalar.copy)
+        back(*chunks[1], 0, PACK, nc.vector.tensor_copy)
+        quantise_features(*chunks[0])
+        back(*chunks[2], 0, PACK, nc.scalar.copy)
+        quantise_features(*chunks[1])
+        back(*chunks[3], 0, 2, nc.vector.tensor_copy)
+        quantise_features(*chunks[2])
+        back(*chunks[3], 2, PACK, nc.scalar.copy)
+        quantise_features(*chunks[3])
 
         scores = score_pool.tile([P, TOKENS], F32, name="scores")
         for g in range(PASSES):

from contextlib import ExitStack
import math

import concourse.masks as masks
import concourse.mybir as mybir

F32 = mybir.dt.float32
BF16 = mybir.dt.bfloat16
U32 = mybir.dt.uint32
U8 = mybir.dt.uint8
FP8X4 = mybir.dt.float8_e4m3fn_x4

P = 128
PACK = 4
K_PASS = P * PACK
BATCH, SEQ, D = 2, 64, 1024
TOKENS = BATCH * SEQ
PASSES = D // K_PASS
WORDS = D // 2
BLOCKS = WORDS // P
INV_SQRT = 1.0 / math.sqrt(D // 8)

FLOPS = 2 * 2 * TOKENS * D * D + 2 * BATCH * SEQ * SEQ * D


def tile_attentionnet_pa_s_kernel(tc, x, wq, wk, out):
    nc = tc.nc
    weights = {"q": wq, "k": wk}
    with ExitStack() as ctx:
        keep = ctx.enter_context(tc.tile_pool(name="keep", bufs=1))
        turned_pool = ctx.enter_context(tc.psum_pool(name="turned", bufs=7))
        score_pool = ctx.enter_context(tc.psum_pool(name="score", bufs=1))
        ctx.enter_context(tc.manual_schedule())

        x_rows = keep.tile([P, D], BF16, name="x_rows")
        x_grouped = keep.tile([P, D], BF16, name="x_grouped", align_bytes=64)
        x_codes = keep.tile([P, PASSES, TOKENS], U32, name="x_codes", align_bytes=64)
        x_scales = keep.tile([P, PASSES, TOKENS], U8, name="x_scales", align_bytes=64)
        w_rows, w_grouped, w_codes, w_scales = {}, {}, {}, {}
        f_grouped, f_codes, f_scales = {}, {}, {}
        for n in weights:
            w_rows[n] = keep.tile([P, PASSES, PACK, D], BF16, name="rows_" + n)
            w_grouped[n] = keep.tile([P, PASSES, PACK, D], BF16, name="grouped_" + n, align_bytes=64)
            w_codes[n] = keep.tile([P, PASSES, PACK, PASSES, P], U32, name="codes_" + n, align_bytes=64)
            w_scales[n] = keep.tile([P, PASSES, PACK, PASSES, P], U8, name="scales_" + n, align_bytes=64)
            f_grouped[n] = keep.tile([P, PASSES, TOKENS, PACK], BF16, name="fgrouped_" + n, align_bytes=64)
            f_codes[n] = keep.tile([P, PASSES, TOKENS], U32, name="fcodes_" + n, align_bytes=64)
            f_scales[n] = keep.tile([P, PASSES, TOKENS], U8, name="fscales_" + n, align_bytes=64)

        nc.sync.dma_start(out=x_rows[:], in_=x.rearrange("b s d -> (b s) d"))
        chunks = [(n, g) for g in range(PASSES) for n in ("q", "k")]
        for n, g in chunks:
            view = weights[n].rearrange("(g p t) d -> p g t d", g=PASSES, p=P, t=PACK)
            for t in range(0, PACK, 2):
                nc.sync.dma_start(out=w_rows[n][:, g, t : t + 2, :], in_=view[:, g, t : t + 2, :])

        ident = keep.tile([P, P], F32, name="ident")
        masks.make_identity(nc, ident[:])

        zero = keep.tile([P, 1], F32, name="zero")
        one = keep.tile([P, 1], F32, name="one")
        nc.vector.memset(zero[:], 0.0)
        nc.scalar.activation(out=one[:], in_=zero[:], func=mybir.ActivationFunctionType.Exp)

        def turn(rows, grouped, copy):
            turned = turned_pool.tile([P, BLOCKS, P], F32, name="turned")
            words = rows.bitcast(F32)
            for c in range(PASSES):
                for u in range(2):
                    picked = words[:, c * 2 * P + u : (c + 1) * 2 * P : 2]
                    nc.tensor.transpose(turned[:, 2 * c + u, :], picked, ident[:])
            copy(
                out=grouped.bitcast(F32).rearrange("p (c m u) -> p c m u", c=PASSES, u=2),
                in_=turned[:].rearrange("p (c u) m -> p c m u", u=2),
            )

        def quantise(grouped, codes, scales):
            nc.vector.quantize_mx(out=codes.bitcast(FP8X4), scales=scales, in_=grouped)

        def front(n, g):
            for t in range(PACK):
                copy = nc.vector.tensor_copy if t == 1 else nc.scalar.copy
                turn(w_rows[n][:, g, t, :], w_grouped[n][:, g, t, :], copy)
                if t > 0:
                    quantise_rows(n, g, t - 1)
            quantise_rows(n, g, PACK - 1)

        def quantise_rows(n, g, t):
            quantise(
                w_grouped[n][:, g, t, :],
                w_codes[n][:, g, t, :, :].rearrange("p c m -> p (c m)"),
                w_scales[n][:, g, t, :, :].rearrange("p c m -> p (c m)"),
            )

        def last_front(n, g):
            for t in range(PACK - 1):
                copy = nc.vector.tensor_copy if t == 1 else nc.scalar.copy
                turn(w_rows[n][:, g, t, :], w_grouped[n][:, g, t, :], copy)
                if t > 0:
                    quantise_rows(n, g, t - 1)
            t = PACK - 1
            words = w_rows[n][:, g, t, :].bitcast(F32)
            grouped = w_grouped[n][:, g, t, :].rearrange("p (c k) -> p c k", c=PASSES)
            halves = []
            for c in range(PASSES):
                turned = turned_pool.tile([P, BLOCKS, P], F32, name="turned")
                for u in range(2):
                    picked = words[:, c * 2 * P + u : (c + 1) * 2 * P : 2]
                    nc.tensor.transpose(turned[:, u, :], picked, ident[:])
                halves.append(turned)
            for c, copy in enumerate((nc.vector.tensor_copy, nc.scalar.copy)):
                copy(
                    out=grouped[:, c, :].bitcast(F32).rearrange("p (m u) -> p m u", u=2),
                    in_=halves[c][:, 0:2, :].rearrange("p u m -> p m u"),
                )
            quantise_rows(n, g, t - 1)
            for c in range(PASSES):
                quantise(grouped[:, c, :], w_codes[n][:, g, t, c, :], w_scales[n][:, g, t, c, :])

        def quantise_features(n, g):
            quantise(
                f_grouped[n][:, g, :, :].rearrange("p n t -> p (n t)"),
                f_codes[n][:, g, :],
                f_scales[n][:, g, :],
            )

        def project(n, g, t, out):
            for c in range(PASSES):
                nc.tensor.matmul_mx(
                    out=out,
                    lhsT=w_codes[n][:, g, t, c, :].bitcast(FP8X4),
                    lhsT_scale=w_scales[n][:, g, t, c, :],
                    rhs=x_codes[:, c, :].bitcast(FP8X4),
                    rhs_scale=x_scales[:, c, :],
                    start=(c == 0),
                    stop=(c == PASSES - 1),
                )

        def back(n, g, t0, t1, copy):
            proj = turned_pool.tile([P, BLOCKS, P], F32, name="turned")
            for t in range(t0, t1):
                project(n, g, t, proj[:, t - t0, :])
            copy(
                out=f_grouped[n][:, g, :, t0:t1],
                in_=proj[:, 0 : t1 - t0, :].rearrange("p t n -> p n t"),
            )

        turn(x_rows[:], x_grouped[:], nc.vector.tensor_copy)
        quantise(
            x_grouped[:],
            x_codes[:].rearrange("p c m -> p (c m)"),
            x_scales[:].rearrange("p c m -> p (c m)"),
        )
        front(*chunks[0])
        for i in range(1, len(chunks)):
            (front if i < len(chunks) - 1 else last_front)(*chunks[i])
        back(*chunks[0], 0, PACK, nc.scalar.copy)
        back(*chunks[1], 0, PACK, nc.vector.tensor_copy)
        quantise_features(*chunks[0])
        back(*chunks[2], 0, PACK, nc.scalar.copy)
        quantise_features(*chunks[1])
        back(*chunks[3], 0, 2, nc.vector.tensor_copy)
        quantise_features(*chunks[2])
        back(*chunks[3], 2, PACK, nc.scalar.copy)
        quantise_features(*chunks[3])

        scores = score_pool.tile([P, TOKENS], F32, name="scores")
        for g in range(PASSES):
            nc.tensor.matmul_mx(
                out=scores[:],
                lhsT=f_codes["q"][:, g, :].bitcast(FP8X4),
                lhsT_scale=f_scales["q"][:, g, :],
                rhs=f_codes["k"][:, g, :].bitcast(FP8X4),
                rhs_scale=f_scales["k"][:, g, :],
                start=(g == 0),
                stop=(g == PASSES - 1),
            )

        scaled = keep.tile([P, SEQ], F32, name="scaled")
        neg_max = keep.tile([P, 1], F32, name="neg_max")
        for b in range(BATCH):
            rows = slice(b * SEQ, (b + 1) * SEQ)
            nc.vector.tensor_scalar(
                out=scaled[rows, :],
                in0=scores[rows, rows],
                scalar1=-INV_SQRT,
                scalar2=None,
                op0=mybir.AluOpType.mult,
                op1=mybir.AluOpType.min,
                accum_out=neg_max[rows, :],
            )
        expd = keep.tile([P, SEQ], F32, name="expd")
        row_sum = keep.tile([P, 1], F32, name="row_sum")
        nc.scalar.activation(
            out=expd[:],
            in_=scaled[:],
            func=mybir.ActivationFunctionType.Exp,
            bias=neg_max[:, 0:1],
            scale=-1.0,
            accum_out=row_sum[:],
        )
        inv_sum = keep.tile([P, 1], F32, name="inv_sum")
        nc.vector.reciprocal(out=inv_sum[:], in_=row_sum[:])
        prob = keep.tile([P, SEQ], F32, name="prob")
        nc.vector.tensor_scalar_mul(out=prob[:], in0=expd[:], scalar1=inv_sum[:, 0:1])
        nc.sync.dma_start(out=out.rearrange("b s k -> (b s) k"), in_=prob[:])
